import numpy as np
import ml_dtypes


def mxq(x, axis, fmt="e4m3"):
    dtype, down = {"e4m3": (ml_dtypes.float8_e4m3fn, 7), "e5m2": (ml_dtypes.float8_e5m2, 14)}[fmt]
    v = np.moveaxis(np.asarray(x, np.float32).astype(ml_dtypes.bfloat16).astype(np.float64), axis, -1)
    blocks = v.reshape(v.shape[:-1] + (-1, 32))
    amax = np.abs(blocks).max(-1, keepdims=True)
    byte = np.maximum(np.where(amax > 0, np.frexp(amax)[1] - 1 + 127, 0) - down, 1)
    scale = np.exp2(byte - 127.0)
    codes = (blocks / scale).astype(np.float32).astype(dtype).astype(np.float64)
    return np.moveaxis((codes * scale).reshape(v.shape), -1, axis)


WIDE = False


def mx_kscale(k):
    if not WIDE:
        return np.ones(k)
    levels = np.array([30, -30])
    if k % 512:
        return np.exp2(np.random.permutation(np.resize(levels, k // 32))).repeat(32)
    a = np.empty((k // 512, 16))
    for p in range(k // 512):
        a[p, :8] = np.random.permutation(np.resize(levels, 8))
        for g in range(8):
            far = levels[np.abs(levels - a[p, g]) >= 10]
            a[p, g + 8] = far[np.random.randint(len(far))]
    return np.exp2(a.ravel()).repeat(32)


BF16 = ml_dtypes.bfloat16


def bf(x):
    return np.asarray(x, np.float32).astype(BF16)


def f64(x):
    return np.asarray(x).astype(np.float64)


M, K, N = 2048, 1024, 512
EPS = 1e-05


def setup_inputs():
    s = mx_kscale(K)
    return {"x": bf(np.random.standard_normal((M, K)) * s),
            "weight": bf(np.random.standard_normal((N, K)) / np.sqrt(K) / s[None, :]),
            "bias": bf(np.random.standard_normal(N) * 0.5),
            "gamma": bf(1.0 + 0.1 * np.random.standard_normal(N)),
            "beta": bf(0.1 * np.random.standard_normal(N)),
            "scale": bf(2.0 + 0.1 * np.random.standard_normal(1))}


def reference(x, weight, bias, gamma, beta, scale):
    acc = (mxq(f64(x), 1, "e5m2") @ mxq(f64(weight), 1, "e5m2").T) + f64(bias)[None, :]
    mean = np.mean(acc, axis=1, keepdims=True)
    var = np.mean((acc - mean) ** 2, axis=1, keepdims=True)
    normalized = (acc - mean) / np.sqrt(var + EPS)
    scaled = (normalized * f64(gamma)[None, :] + f64(beta)[None, :]) * f64(scale)[0]
    e = np.exp(scaled - scaled.max(axis=1, keepdims=True))
    return e / e.sum(axis=1, keepdims=True)

@@ -1,0 +1,268 @@
+from contextlib import ExitStack
+
+import concourse.mybir as mybir
+from concourse.masks import make_identity
+
+M, K, N = 2048, 1024, 512
+EPS = 1e-05
+FLOPS = 2 * M * K * N
+
+F32 = mybir.dt.float32
+BF16 = mybir.dt.bfloat16
+U32 = mybir.dt.uint32
+U8 = mybir.dt.uint8
+E5X4 = mybir.dt.float8_e5m2_x4
+ALU = mybir.AluOpType
+ACT = mybir.ActivationFunctionType
+
+P = 128
+NT = M // P
+NW = N // P
+G = K // 512
+NB1 = 12
+
+
+def tile_modelnew_kernel(tc, x, weight, bias, gamma, beta, scale, out):
+    nc = tc.nc
+    x_t = x.rearrange("(i p) k -> i p k", p=P)
+    w_t = weight.rearrange("(j p) k -> j p k", p=P)
+    out_t = out.rearrange("(i p) n -> i p n", p=P)
+
+    with ExitStack() as ctx:
+        const = ctx.enter_context(tc.tile_pool(name="const", bufs=1))
+        xin = ctx.enter_context(tc.tile_pool(name="xin", bufs=NT))
+        win = ctx.enter_context(tc.tile_pool(name="win", bufs=NW))
+        work = ctx.enter_context(tc.tile_pool(name="work", bufs=4))
+        keep = ctx.enter_context(tc.tile_pool(name="keep", bufs=NT))
+        psum = ctx.enter_context(tc.psum_pool(name="psum", bufs=3))
+        pconst = ctx.enter_context(tc.psum_pool(name="pconst", bufs=1))
+        ctx.enter_context(tc.manual_schedule())
+
+        ident = const.tile([P, P], F32, name="ident")
+        ones = const.tile([P, P], BF16, name="ones")
+        vrow = const.tile([P, 3, N], BF16, name="vrow")
+        srow = const.tile([P, 2], BF16, name="srow")
+        nsc_mat = const.tile([P, P], BF16, name="nsc_mat")
+        warm = const.tile([P, 4], F32, name="warm")
+        nscale = const.tile([P, 1], F32, name="nscale")
+        bias_bc = const.tile([P, N], F32, name="bias_bc")
+        gpn = pconst.tile([P, N], F32, name="gpn")
+        nbp = pconst.tile([P, N], F32, name="nbp")
+        sums = const.tile([P, NT], F32, name="sums")
+        negmean = const.tile([P, NT], F32, name="negmean")
+        ssq = const.tile([P, NT], F32, name="ssq")
+        std = const.tile([P, NT], F32, name="std")
+        rstd = const.tile([P, NT], F32, name="rstd")
+        negm = const.tile([P, NT], F32, name="negm")
+        esum = const.tile([P, NT], F32, name="esum")
+        rsum = const.tile([P, NT], F32, name="rsum")
+        wgrp = const.tile([P, G * N * 4], BF16, name="wgrp", align_bytes=64)
+        wcodes = const.tile([P, G * N], U32, name="wcodes", align_bytes=64)
+        wscl = const.tile([P, G * N], U8, name="wscl", align_bytes=64)
+
+        nc.vector.memset(srow[:], 0.0)
+        nc.vector.memset(warm[:], 0.0)
+        nc.vector.memset(ones[:], 1.0)
+        nc.vector.memset(vrow[:], 0.0)
+        make_identity(nc, ident[:])
+        nc.scalar.activation(out=warm[:, 1:2], in_=warm[:, 0:1], func=ACT.Square)
+
+        x_sb = {}
+        w_sb = {}
+
+        def load_x(i):
+            x_sb[i] = xin.tile([P, K], BF16, name="x_sb", tag="x_sb")
+            nc.sync.dma_start(out=x_sb[i][:], in_=x_t[i])
+
+        def load_w(j):
+            w_sb[j] = win.tile([P, K], BF16, name="w_sb", tag="w_sb")
+            nc.sync.dma_start(out=w_sb[j][:], in_=w_t[j])
+
+        load_x(0)
+        nc.sync.dma_start(out=srow[0:1, 0:1], in_=scale.rearrange("(o n) -> o n", o=1))
+        for j in range(NW):
+            load_w(j)
+        nc.sync.dma_start(out=vrow[0:1, 0, :], in_=bias.rearrange("(o n) -> o n", o=1))
+        nc.sync.dma_start(out=vrow[0:1, 1, :], in_=gamma.rearrange("(o n) -> o n", o=1))
+        nc.sync.dma_start(out=vrow[0:1, 2, :], in_=beta.rearrange("(o n) -> o n", o=1))
+        for i in range(1, NT):
+            load_x(i)
+
+        xt = {}
+        grp = {}
+        codes = {}
+        scl = {}
+        acc = {}
+        h = {}
+        t2 = {}
+        sneg = {}
+        e = {}
+
+        def transposes(src):
+            bank = psum.tile([P, 512], F32, name="xt", tag="xt")
+            words = src[:].bitcast(F32)
+            for g in range(G):
+                for u in range(2):
+                    q = 2 * g + u
+                    nc.tensor.transpose(
+                        bank[:, q * P:(q + 1) * P],
+                        words[:, 256 * g + u:256 * (g + 1):2],
+                        ident[:],
+                    )
+            return bank
+
+        def st_T(i):
+            xt[i] = transposes(x_sb[i])
+
+        def st_CP(i):
+            grp[i] = work.tile([P, K], BF16, name="grp", tag="grp", align_bytes=64)
+            nc.scalar.copy(
+                out=grp[i][:].bitcast(F32).rearrange("p (g r u) -> p g r u", g=G, u=2),
+                in_=xt[i][:].rearrange("p (g u r) -> p g r u", g=G, u=2),
+            )
+
+        def st_Q(i):
+            codes[i] = work.tile([P, K // 4], U32, name="codes", tag="codes", align_bytes=64)
+            scl[i] = work.tile([P, K // 4], U8, name="scl", tag="scl", align_bytes=64)
+            nc.vector.quantize_mx(out=codes[i][:].bitcast(E5X4), scales=scl[i][:], in_=grp[i][:])
+
+        def st_MM(i):
+            acc[i] = psum.tile([P, N], F32, name="acc", tag="acc")
+            for g in range(G):
+                nc.tensor.matmul_mx(
+                    out=acc[i][:],
+                    lhsT=codes[i][:, g * P:(g + 1) * P].bitcast(E5X4),
+                    lhsT_scale=scl[i][:, g * P:(g + 1) * P],
+                    rhs=wcodes[:, g * N:(g + 1) * N].bitcast(E5X4),
+                    rhs_scale=wscl[:, g * N:(g + 1) * N],
+                    start=(g == 0),
+                    stop=(g == G - 1),
+                )
+
+        def st_A(i):
+            h[i] = work.tile([P, N], F32, name="h", tag="h")
+            nc.vector.scalar_tensor_tensor(
+                out=h[i][:], in0=acc[i][:], scalar=1.0, in1=bias_bc[:],
+                op0=ALU.mult, op1=ALU.add, accum_out=sums[:, i:i + 1],
+            )
+
+        def st_SQ(i):
+            nc.scalar.mul(out=negmean[:, i:i + 1], in_=sums[:, i:i + 1], mul=-1.0 / N)
+            junk = work.tile([P, N], F32, name="junk", tag="junk", bufs=2)
+            nc.scalar.activation(
+                out=junk[:], in_=h[i][:], func=ACT.Square,
+                bias=negmean[:, i:i + 1], scale=1.0, accum_out=ssq[:, i:i + 1],
+            )
+
+        def st_B(i):
+            t2[i] = keep.tile([P, N], F32, name="t2", tag="t2")
+            nc.vector.scalar_tensor_tensor(
+                out=t2[i][:], in0=h[i][:], scalar=negmean[:, i:i + 1], in1=gpn[:],
+                op0=ALU.add, op1=ALU.mult,
+            )
+
+        def st_C(i):
+            sneg[i] = work.tile([P, N], F32, name="sneg", tag="sneg")
+            nc.vector.scalar_tensor_tensor(
+                out=sneg[i][:], in0=t2[i][:], scalar=rstd[:, i:i + 1], in1=nbp[:],
+                op0=ALU.mult, op1=ALU.add,
+            )
+
+        def st_D(i):
+            nc.vector.tensor_reduce(
+                out=negm[:, i:i + 1], in_=sneg[i][:], axis=mybir.AxisListType.X, op=ALU.min,
+            )
+
+        def st_E(i):
+            e[i] = work.tile([P, N], F32, name="e", tag="e", bufs=6)
+            nc.scalar.activation(
+                out=e[i][:], in_=sneg[i][:], func=ACT.Exp,
+                bias=negm[:, i:i + 1], scale=-1.0, accum_out=esum[:, i:i + 1],
+            )
+
+        def st_R(i, n):
+            nc.vector.reciprocal(out=rsum[:, i:i + n], in_=esum[:, i:i + n])
+
+        def st_F(i):
+            if i == NT - 1:
+                nc.vector.tensor_scalar(out=e[i][:], in0=e[i][:], scalar1=rsum[:, i:i + 1], scalar2=None, op0=ALU.mult)
+            else:
+                nc.scalar.activation(out=e[i][:], in_=e[i][:], func=ACT.Copy, scale=rsum[:, i:i + 1])
+            nc.sync.dma_start(out=out_t[i], in_=e[i][:])
+
+        def ok(i):
+            return 0 <= i < NT
+
+        st_T(0)
+        st_CP(0)
+        st_Q(0)
+        wgrp_w = wgrp[:].bitcast(F32).rearrange("p (g c u) -> p g c u", g=G, u=2)
+        for j in range(NW):
+            wbank = transposes(w_sb[j])
+            nc.scalar.copy(
+                out=wgrp_w[:, :, j * P:(j + 1) * P, :],
+                in_=wbank[:].rearrange("p (g u r) -> p g r u", g=G, u=2),
+            )
+            for g in range(G):
+                c0 = g * N + j * P
+                nc.vector.quantize_mx(
+                    out=wcodes[:, c0:c0 + P].bitcast(E5X4),
+                    scales=wscl[:, c0:c0 + P],
+                    in_=wgrp[:, 4 * c0:4 * (c0 + P)],
+                )
+            if j == 1:
+                ps_s = psum.tile([P, N], F32, name="ps_s", tag="acc")
+                nc.tensor.matmul(out=ps_s[:, 0:2], lhsT=ones[:], rhs=srow[:], start=True, stop=True)
+                nc.vector.tensor_scalar(out=nscale[:], in0=ps_s[:, 0:1], scalar1=-1.0, scalar2=None, op0=ALU.mult)
+                nc.vector.tensor_scalar(out=nsc_mat[:], in0=ones[:], scalar1=nscale[:, 0:1], scalar2=None, op0=ALU.mult)
+        ps_b = psum.tile([P, N], F32, name="ps_b", tag="acc")
+        nc.tensor.matmul(out=ps_b[:], lhsT=ones[:], rhs=vrow[:, 0, :], start=True, stop=True)
+        nc.vector.tensor_copy(out=bias_bc[:], in_=ps_b[:])
+        st_T(1)
+
+        for k in range(-4, NT):
+            if k % 2 == 0:
+                for i in (k + 2, k + 3):
+                    if ok(i):
+                        st_MM(i)
+                if k == -2:
+                    nc.tensor.matmul(out=gpn[:], lhsT=nsc_mat[:], rhs=vrow[:, 1, :], start=True, stop=True)
+                    nc.tensor.matmul(out=nbp[:], lhsT=nsc_mat[:], rhs=vrow[:, 2, :], start=True, stop=True)
+                for i in (k + 6, k + 7):
+                    if ok(i):
+                        st_T(i)
+            if ok(k + 5) and k + 5 >= 1:
+                st_CP(k + 5)
+            if ok(k + 1):
+                st_A(k + 1)
+                st_SQ(k + 1)
+            if k + 1 == NB1 - 1:
+                nc.scalar.activation(out=std[:, 0:NB1], in_=ssq[:, 0:NB1], func=ACT.Sqrt, bias=EPS, scale=1.0 / N)
+            if k + 1 == NT - 1:
+                nc.scalar.activation(out=std[:, NB1:NT], in_=ssq[:, NB1:NT], func=ACT.Sqrt, bias=EPS, scale=1.0 / N)
+                nc.scalar.activation(out=warm[:, 2:3], in_=warm[:, 0:1], func=ACT.Exp)
+            if ok(k):
+                st_B(k)
+            if k == NB1 + 1:
+                nc.vector.reciprocal(out=rstd[:, 0:NB1], in_=std[:, 0:NB1])
+            if ok(k + 4) and k + 4 >= 1:
+                st_Q(k + 4)
+
+        for i in range(-1, NT + 1):
+            if ok(i + 1):
+                st_C(i + 1)
+            if ok(i):
+                st_D(i)
+                st_E(i)
+            if i == 2:
+                nc.vector.reciprocal(out=rstd[:, NB1:NT], in_=std[:, NB1:NT])
+            if i >= 2 and i % 2 == 0 and i < NT:
+                st_R(i - 2, 2)
+                st_F(i - 2)
+                st_F(i - 1)
+            if i == NT - 1:
+                st_R(NT - 2, 1)
+                st_F(NT - 2)
+            if i == NT:
+                st_R(NT - 1, 1)
+                st_F(NT - 1)

@@ -20,6 +20,8 @@ NT = M // P
 NW = N // P
 G = K // 512
 NB1 = 12
+G_TILES = (1, 3, 5, 7, 9, 11, 13)
+G_AHEAD = 4
 
 
 def tile_modelnew_kernel(tc, x, weight, bias, gamma, beta, scale, out):
@@ -46,6 +48,7 @@ def tile_modelnew_kernel(tc, x, weight, bias, gamma, beta, scale, out):
         warm = const.tile([P, 4], F32, name="warm")
         nscale = const.tile([P, 1], F32, name="nscale")
         bias_bc = const.tile([P, N], F32, name="bias_bc")
+        nbp_sb = const.tile([P, N], F32, name="nbp_sb")
         gpn = pconst.tile([P, N], F32, name="gpn")
         nbp = pconst.tile([P, N], F32, name="nbp")
         sums = const.tile([P, NT], F32, name="sums")
@@ -168,13 +171,21 @@ def tile_modelnew_kernel(tc, x, weight, bias, gamma, beta, scale, out):
                 op0=ALU.mult, op1=ALU.add,
             )
 
+        def st_CG(i):
+            sneg[i] = keep.tile([P, N], F32, name="sneg_g", tag="sneg_g", bufs=len(G_TILES))
+            nc.gpsimd.tensor_scalar(
+                out=sneg[i][:], in0=t2[i][:], scalar1=rstd[:, i:i + 1], scalar2=0.0,
+                op0=ALU.mult, op1=ALU.add,
+            )
+            nc.gpsimd.tensor_tensor(out=sneg[i][:], in0=sneg[i][:], in1=nbp_sb[:], op=ALU.add)
+
         def st_D(i):
             nc.vector.tensor_reduce(
                 out=negm[:, i:i + 1], in_=sneg[i][:], axis=mybir.AxisListType.X, op=ALU.min,
             )
 
         def st_E(i):
-            e[i] = work.tile([P, N], F32, name="e", tag="e", bufs=6)
+            e[i] = work.tile([P, N], F32, name="e", tag="e", bufs=8)
             nc.scalar.activation(
                 out=e[i][:], in_=sneg[i][:], func=ACT.Exp,
                 bias=negm[:, i:i + 1], scale=-1.0, accum_out=esum[:, i:i + 1],
@@ -186,6 +197,11 @@ def tile_modelnew_kernel(tc, x, weight, bias, gamma, beta, scale, out):
         def st_F(i):
             if i == NT - 1:
                 nc.vector.tensor_scalar(out=e[i][:], in0=e[i][:], scalar1=rsum[:, i:i + 1], scalar2=None, op0=ALU.mult)
+            elif i in G_TILES:
+                nc.gpsimd.tensor_scalar(
+                    out=e[i][:], in0=e[i][:], scalar1=rsum[:, i:i + 1], scalar2=0.0,
+                    op0=ALU.mult, op1=ALU.add,
+                )
             else:
                 nc.scalar.activation(out=e[i][:], in_=e[i][:], func=ACT.Copy, scale=rsum[:, i:i + 1])
             nc.sync.dma_start(out=out_t[i], in_=e[i][:])
@@ -228,6 +244,7 @@ def tile_modelnew_kernel(tc, x, weight, bias, gamma, beta, scale, out):
                 if k == -2:
                     nc.tensor.matmul(out=gpn[:], lhsT=nsc_mat[:], rhs=vrow[:, 1, :], start=True, stop=True)
                     nc.tensor.matmul(out=nbp[:], lhsT=nsc_mat[:], rhs=vrow[:, 2, :], start=True, stop=True)
+                    nc.scalar.copy(out=nbp_sb[:], in_=nbp[:])
                 for i in (k + 6, k + 7):
                     if ok(i):
                         st_T(i)
@@ -245,11 +262,13 @@ def tile_modelnew_kernel(tc, x, weight, bias, gamma, beta, scale, out):
                 st_B(k)
             if k == NB1 + 1:
                 nc.vector.reciprocal(out=rstd[:, 0:NB1], in_=std[:, 0:NB1])
+                for i in G_TILES[0:G_AHEAD]:
+                    st_CG(i)
             if ok(k + 4) and k + 4 >= 1:
                 st_Q(k + 4)
 
         for i in range(-1, NT + 1):
-            if ok(i + 1):
+            if ok(i + 1) and i + 1 not in G_TILES:
                 st_C(i + 1)
             if ok(i):
                 st_D(i)
@@ -260,6 +279,9 @@ def tile_modelnew_kernel(tc, x, weight, bias, gamma, beta, scale, out):
                 st_R(i - 2, 2)
                 st_F(i - 2)
                 st_F(i - 1)
+                g_next = G_AHEAD + i // 2 - 1
+                if g_next < len(G_TILES):
+                    st_CG(G_TILES[g_next])
             if i == NT - 1:
                 st_R(NT - 2, 1)
                 st_F(NT - 2)

@@ -20,8 +20,12 @@ NT = M // P
 NW = N // P
 G = K // 512
 NB1 = 12
-G_TILES = (1, 3, 5, 7, 9, 11, 13)
-G_AHEAD = 4
+GB = (13, 14, 15)
+FG = (8, 9, 10, 11, 12, 13)
+FV = (14, 15)
+RL = 3
+N_WARM = 4
+N_KEEP = 2
 
 
 def tile_modelnew_kernel(tc, x, weight, bias, gamma, beta, scale, out):
@@ -45,9 +49,13 @@ def tile_modelnew_kernel(tc, x, weight, bias, gamma, beta, scale, out):
         vrow = const.tile([P, 3, N], BF16, name="vrow")
         srow = const.tile([P, 2], BF16, name="srow")
         nsc_mat = const.tile([P, P], BF16, name="nsc_mat")
+        zrow = const.tile([P, N], BF16, name="zrow")
         warm = const.tile([P, 4], F32, name="warm")
         nscale = const.tile([P, 1], F32, name="nscale")
         bias_bc = const.tile([P, N], F32, name="bias_bc")
+        gam_bf = const.tile([P, N], BF16, name="gam_bf")
+        bet_bf = const.tile([P, N], BF16, name="bet_bf")
+        gpn_sb = const.tile([P, N], F32, name="gpn_sb")
         nbp_sb = const.tile([P, N], F32, name="nbp_sb")
         gpn = pconst.tile([P, N], F32, name="gpn")
         nbp = pconst.tile([P, N], F32, name="nbp")
@@ -55,6 +63,7 @@ def tile_modelnew_kernel(tc, x, weight, bias, gamma, beta, scale, out):
         negmean = const.tile([P, NT], F32, name="negmean")
         ssq = const.tile([P, NT], F32, name="ssq")
         std = const.tile([P, NT], F32, name="std")
+        mhalf = const.tile([P, NT], F32, name="mhalf")
         rstd = const.tile([P, NT], F32, name="rstd")
         negm = const.tile([P, NT], F32, name="negm")
         esum = const.tile([P, NT], F32, name="esum")
@@ -63,12 +72,14 @@ def tile_modelnew_kernel(tc, x, weight, bias, gamma, beta, scale, out):
         wcodes = const.tile([P, G * N], U32, name="wcodes", align_bytes=64)
         wscl = const.tile([P, G * N], U8, name="wscl", align_bytes=64)
 
+        nc.vector.memset(ones[:], 1.0)
+        nc.vector.memset(zrow[:], 0.0)
         nc.vector.memset(srow[:], 0.0)
         nc.vector.memset(warm[:], 0.0)
-        nc.vector.memset(ones[:], 1.0)
+        nc.vector.memset(mhalf[:], -0.5)
         nc.vector.memset(vrow[:], 0.0)
         make_identity(nc, ident[:])
-        nc.scalar.activation(out=warm[:, 1:2], in_=warm[:, 0:1], func=ACT.Square)
+        nc.scalar.activation(out=warm[:, 1:2], in_=warm[:, 0:1], func=ACT.Exp)
 
         x_sb = {}
         w_sb = {}
@@ -90,6 +101,8 @@ def tile_modelnew_kernel(tc, x, weight, bias, gamma, beta, scale, out):
         nc.sync.dma_start(out=vrow[0:1, 2, :], in_=beta.rearrange("(o n) -> o n", o=1))
         for i in range(1, NT):
             load_x(i)
+        nc.sync.dma_start(out=gam_bf[:], in_=gamma.partition_broadcast(P))
+        nc.sync.dma_start(out=bet_bf[:], in_=beta.partition_broadcast(P))
 
         xt = {}
         grp = {}
@@ -143,7 +156,10 @@ def tile_modelnew_kernel(tc, x, weight, bias, gamma, beta, scale, out):
                 )
 
         def st_A(i):
-            h[i] = work.tile([P, N], F32, name="h", tag="h")
+            if i in GB:
+                h[i] = keep.tile([P, N], F32, name="hg", tag="hg", bufs=len(GB))
+            else:
+                h[i] = work.tile([P, N], F32, name="h", tag="h")
             nc.vector.scalar_tensor_tensor(
                 out=h[i][:], in0=acc[i][:], scalar=1.0, in1=bias_bc[:],
                 op0=ALU.mult, op1=ALU.add, accum_out=sums[:, i:i + 1],
@@ -171,12 +187,13 @@ def tile_modelnew_kernel(tc, x, weight, bias, gamma, beta, scale, out):
                 op0=ALU.mult, op1=ALU.add,
             )
 
-        def st_CG(i):
-            sneg[i] = keep.tile([P, N], F32, name="sneg_g", tag="sneg_g", bufs=len(G_TILES))
+        def st_BCG(i):
+            sneg[i] = keep.tile([P, N], F32, name="sneg_g", tag="sneg_g", bufs=len(GB))
             nc.gpsimd.tensor_scalar(
-                out=sneg[i][:], in0=t2[i][:], scalar1=rstd[:, i:i + 1], scalar2=0.0,
-                op0=ALU.mult, op1=ALU.add,
+                out=sneg[i][:], in0=h[i][:], scalar1=negmean[:, i:i + 1], scalar2=rstd[:, i:i + 1],
+                op0=ALU.add, op1=ALU.mult,
             )
+            nc.gpsimd.tensor_tensor(out=sneg[i][:], in0=sneg[i][:], in1=gpn_sb[:], op=ALU.mult)
             nc.gpsimd.tensor_tensor(out=sneg[i][:], in0=sneg[i][:], in1=nbp_sb[:], op=ALU.add)
 
         def st_D(i):
@@ -185,7 +202,7 @@ def tile_modelnew_kernel(tc, x, weight, bias, gamma, beta, scale, out):
             )
 
         def st_E(i):
-            e[i] = work.tile([P, N], F32, name="e", tag="e", bufs=8)
+            e[i] = work.tile([P, N], F32, name="e", tag="e", bufs=10)
             nc.scalar.activation(
                 out=e[i][:], in_=sneg[i][:], func=ACT.Exp,
                 bias=negm[:, i:i + 1], scale=-1.0, accum_out=esum[:, i:i + 1],
@@ -195,9 +212,9 @@ def tile_modelnew_kernel(tc, x, weight, bias, gamma, beta, scale, out):
             nc.vector.reciprocal(out=rsum[:, i:i + n], in_=esum[:, i:i + n])
 
         def st_F(i):
-            if i == NT - 1:
+            if i in FV:
                 nc.vector.tensor_scalar(out=e[i][:], in0=e[i][:], scalar1=rsum[:, i:i + 1], scalar2=None, op0=ALU.mult)
-            elif i in G_TILES:
+            elif i in FG:
                 nc.gpsimd.tensor_scalar(
                     out=e[i][:], in0=e[i][:], scalar1=rsum[:, i:i + 1], scalar2=0.0,
                     op0=ALU.mult, op1=ALU.add,
@@ -209,6 +226,12 @@ def tile_modelnew_kernel(tc, x, weight, bias, gamma, beta, scale, out):
         def ok(i):
             return 0 <= i < NT
 
+        def dummy_mm(n):
+            for d in range(n):
+                ps_d = psum.tile([P, N], F32, name="ps_d", tag="acc")
+                nc.tensor.matmul(out=ps_d[:], lhsT=ones[:], rhs=zrow[:], start=True, stop=True)
+
+        dummy_mm(N_WARM)
         st_T(0)
         st_CP(0)
         st_Q(0)
@@ -231,60 +254,52 @@ def tile_modelnew_kernel(tc, x, weight, bias, gamma, beta, scale, out):
                 nc.tensor.matmul(out=ps_s[:, 0:2], lhsT=ones[:], rhs=srow[:], start=True, stop=True)
                 nc.vector.tensor_scalar(out=nscale[:], in0=ps_s[:, 0:1], scalar1=-1.0, scalar2=None, op0=ALU.mult)
                 nc.vector.tensor_scalar(out=nsc_mat[:], in0=ones[:], scalar1=nscale[:, 0:1], scalar2=None, op0=ALU.mult)
+                dummy_mm(N_KEEP)
         ps_b = psum.tile([P, N], F32, name="ps_b", tag="acc")
         nc.tensor.matmul(out=ps_b[:], lhsT=ones[:], rhs=vrow[:, 0, :], start=True, stop=True)
         nc.vector.tensor_copy(out=bias_bc[:], in_=ps_b[:])
         st_T(1)
 
-        for k in range(-4, NT):
-            if k % 2 == 0:
-                for i in (k + 2, k + 3):
-                    if ok(i):
-                        st_MM(i)
-                if k == -2:
-                    nc.tensor.matmul(out=gpn[:], lhsT=nsc_mat[:], rhs=vrow[:, 1, :], start=True, stop=True)
-                    nc.tensor.matmul(out=nbp[:], lhsT=nsc_mat[:], rhs=vrow[:, 2, :], start=True, stop=True)
-                    nc.scalar.copy(out=nbp_sb[:], in_=nbp[:])
-                for i in (k + 6, k + 7):
-                    if ok(i):
-                        st_T(i)
-            if ok(k + 5) and k + 5 >= 1:
-                st_CP(k + 5)
+        for k in range(-3, NT):
+            if ok(k + 2):
+                st_MM(k + 2)
+            if k == -1:
+                nc.tensor.matmul(out=gpn[:], lhsT=nsc_mat[:], rhs=vrow[:, 1, :], start=True, stop=True)
+                nc.tensor.matmul(out=nbp[:], lhsT=nsc_mat[:], rhs=vrow[:, 2, :], start=True, stop=True)
+            if ok(k + 5):
+                st_T(k + 5)
+            if ok(k + 4):
+                st_CP(k + 4)
             if ok(k + 1):
                 st_A(k + 1)
                 st_SQ(k + 1)
             if k + 1 == NB1 - 1:
-                nc.scalar.activation(out=std[:, 0:NB1], in_=ssq[:, 0:NB1], func=ACT.Sqrt, bias=EPS, scale=1.0 / N)
+                nc.gpsimd.tensor_scalar(out=std[:, 0:NB1], in0=ssq[:, 0:NB1], scalar1=1.0 / N, scalar2=EPS, op0=ALU.mult, op1=ALU.add)
+                nc.gpsimd.tensor_tensor(out=rstd[:, 0:NB1], in0=std[:, 0:NB1], in1=mhalf[:, 0:NB1], op=ALU.pow)
             if k + 1 == NT - 1:
-                nc.scalar.activation(out=std[:, NB1:NT], in_=ssq[:, NB1:NT], func=ACT.Sqrt, bias=EPS, scale=1.0 / N)
-                nc.scalar.activation(out=warm[:, 2:3], in_=warm[:, 0:1], func=ACT.Exp)
-            if ok(k):
+                nc.gpsimd.tensor_scalar(out=std[:, NB1:NT], in0=ssq[:, NB1:NT], scalar1=1.0 / N, scalar2=EPS, op0=ALU.mult, op1=ALU.add)
+                nc.gpsimd.tensor_tensor(out=rstd[:, NB1:NT], in0=std[:, NB1:NT], in1=mhalf[:, NB1:NT], op=ALU.pow)
+            if k == 6:
+                nc.gpsimd.tensor_scalar(out=gpn_sb[:], in0=gam_bf[:], scalar1=nscale[:, 0:1], scalar2=0.0, op0=ALU.mult, op1=ALU.add)
+                nc.gpsimd.tensor_scalar(out=nbp_sb[:], in0=bet_bf[:], scalar1=nscale[:, 0:1], scalar2=0.0, op0=ALU.mult, op1=ALU.add)
+            if ok(k) and k not in GB:
                 st_B(k)
-            if k == NB1 + 1:
-                nc.vector.reciprocal(out=rstd[:, 0:NB1], in_=std[:, 0:NB1])
-                for i in G_TILES[0:G_AHEAD]:
-                    st_CG(i)
-            if ok(k + 4) and k + 4 >= 1:
-                st_Q(k + 4)
+            if ok(k + 3) and k + 3 >= 1:
+                st_Q(k + 3)
 
-        for i in range(-1, NT + 1):
-            if ok(i + 1) and i + 1 not in G_TILES:
+        for i in GB:
+            st_BCG(i)
+        for i in range(-1, NT):
+            if ok(i + 1) and i + 1 not in GB:
                 st_C(i + 1)
             if ok(i):
                 st_D(i)
                 st_E(i)
-            if i == 2:
-                nc.vector.reciprocal(out=rstd[:, NB1:NT], in_=std[:, NB1:NT])
-            if i >= 2 and i % 2 == 0 and i < NT:
-                st_R(i - 2, 2)
-                st_F(i - 2)
-                st_F(i - 1)
-                g_next = G_AHEAD + i // 2 - 1
-                if g_next < len(G_TILES):
-                    st_CG(G_TILES[g_next])
-            if i == NT - 1:
-                st_R(NT - 2, 1)
-                st_F(NT - 2)
-            if i == NT:
-                st_R(NT - 1, 1)
-                st_F(NT - 1)
+            j = i - RL
+            if j >= 1 and j % 2 == 1:
+                st_R(j - 1, 2)
+                st_F(j - 1)
+                st_F(j)
+        for j in range(NT - RL - 1, NT):
+            st_R(j, 1)
+            st_F(j)

@@ -21,9 +21,10 @@ NW = N // P
 G = K // 512
 NB1 = 12
 GB = (13, 14, 15)
-FG = (8, 9, 10, 11, 12, 13)
-FV = (14, 15)
-RL = 3
+FG = (7, 8, 9, 10, 11)
+FV = (12, 13, 15)
+NP = NT // 2
+R_AT = {2: (0,), 3: (1,), 4: (2, 3), 5: (4,), 6: (5,)}
 N_WARM = 4
 N_KEEP = 2
 
@@ -58,7 +59,6 @@ def tile_modelnew_kernel(tc, x, weight, bias, gamma, beta, scale, out):
         gpn_sb = const.tile([P, N], F32, name="gpn_sb")
         nbp_sb = const.tile([P, N], F32, name="nbp_sb")
         gpn = pconst.tile([P, N], F32, name="gpn")
-        nbp = pconst.tile([P, N], F32, name="nbp")
         sums = const.tile([P, NT], F32, name="sums")
         negmean = const.tile([P, NT], F32, name="negmean")
         ssq = const.tile([P, NT], F32, name="ssq")
@@ -112,10 +112,12 @@ def tile_modelnew_kernel(tc, x, weight, bias, gamma, beta, scale, out):
         h = {}
         t2 = {}
         sneg = {}
+        sp = {}
+        cst = {}
         e = {}
 
         def transposes(src):
-            bank = psum.tile([P, 512], F32, name="xt", tag="xt")
+            bank = psum.tile([P, 512], F32, name="xt", tag="xt", bufs=4)
             words = src[:].bitcast(F32)
             for g in range(G):
                 for u in range(2):
@@ -180,31 +182,41 @@ def tile_modelnew_kernel(tc, x, weight, bias, gamma, beta, scale, out):
                 op0=ALU.add, op1=ALU.mult,
             )
 
+        def new_sneg(i):
+            if i // 2 not in sp:
+                sp[i // 2] = keep.tile([P, 2, N], F32, name="sp", tag="sp", bufs=NP)
+            sneg[i] = sp[i // 2][:, i % 2, :]
+
         def st_C(i):
-            sneg[i] = work.tile([P, N], F32, name="sneg", tag="sneg")
+            new_sneg(i)
             nc.vector.scalar_tensor_tensor(
-                out=sneg[i][:], in0=t2[i][:], scalar=rstd[:, i:i + 1], in1=nbp[:],
+                out=sneg[i], in0=t2[i][:], scalar=rstd[:, i:i + 1], in1=cst["nbp"][:],
                 op0=ALU.mult, op1=ALU.add,
             )
 
         def st_BCG(i):
-            sneg[i] = keep.tile([P, N], F32, name="sneg_g", tag="sneg_g", bufs=len(GB))
+            new_sneg(i)
             nc.gpsimd.tensor_scalar(
-                out=sneg[i][:], in0=h[i][:], scalar1=negmean[:, i:i + 1], scalar2=rstd[:, i:i + 1],
+                out=sneg[i], in0=h[i][:], scalar1=negmean[:, i:i + 1], scalar2=rstd[:, i:i + 1],
                 op0=ALU.add, op1=ALU.mult,
             )
-            nc.gpsimd.tensor_tensor(out=sneg[i][:], in0=sneg[i][:], in1=gpn_sb[:], op=ALU.mult)
-            nc.gpsimd.tensor_tensor(out=sneg[i][:], in0=sneg[i][:], in1=nbp_sb[:], op=ALU.add)
+            nc.gpsimd.tensor_tensor(out=sneg[i], in0=sneg[i], in1=gpn_sb[:], op=ALU.mult)
+            nc.gpsimd.tensor_tensor(out=sneg[i], in0=sneg[i], in1=nbp_sb[:], op=ALU.add)
 
-        def st_D(i):
+        def st_D(p):
             nc.vector.tensor_reduce(
-                out=negm[:, i:i + 1], in_=sneg[i][:], axis=mybir.AxisListType.X, op=ALU.min,
+                out=negm[:, 2 * p:2 * p + 2], in_=sp[p][:], axis=mybir.AxisListType.X, op=ALU.min,
+            )
+
+        def st_D1(i):
+            nc.vector.tensor_reduce(
+                out=negm[:, i:i + 1], in_=sneg[i], axis=mybir.AxisListType.X, op=ALU.min,
             )
 
         def st_E(i):
-            e[i] = work.tile([P, N], F32, name="e", tag="e", bufs=10)
+            e[i] = work.tile([P, N], F32, name="e", tag="e", bufs=12)
             nc.scalar.activation(
-                out=e[i][:], in_=sneg[i][:], func=ACT.Exp,
+                out=e[i][:], in_=sneg[i], func=ACT.Exp,
                 bias=negm[:, i:i + 1], scale=-1.0, accum_out=esum[:, i:i + 1],
             )
 
@@ -237,10 +249,19 @@ def tile_modelnew_kernel(tc, x, weight, bias, gamma, beta, scale, out):
         st_Q(0)
         wgrp_w = wgrp[:].bitcast(F32).rearrange("p (g c u) -> p g c u", g=G, u=2)
         for j in range(NW):
-            wbank = transposes(w_sb[j])
+            wwords = w_sb[j][:].bitcast(F32)
+            wbank = {}
+            for g in range(G):
+                wbank[g] = psum.tile([P, 512], F32, name="wt", tag="xt", bufs=4)
+                for u in range(2):
+                    nc.tensor.transpose(wbank[g][:, u * P:(u + 1) * P], wwords[:, 256 * g + u:256 * (g + 1):2], ident[:])
             nc.scalar.copy(
-                out=wgrp_w[:, :, j * P:(j + 1) * P, :],
-                in_=wbank[:].rearrange("p (g u r) -> p g r u", g=G, u=2),
+                out=wgrp_w[:, 0, j * P:(j + 1) * P, :],
+                in_=wbank[0][:, 0:2 * P].rearrange("p (u r) -> p r u", u=2),
+            )
+            nc.vector.tensor_copy(
+                out=wgrp_w[:, 1, j * P:(j + 1) * P, :],
+                in_=wbank[1][:, 0:2 * P].rearrange("p (u r) -> p r u", u=2),
             )
             for g in range(G):
                 c0 = g * N + j * P
@@ -265,7 +286,9 @@ def tile_modelnew_kernel(tc, x, weight, bias, gamma, beta, scale, out):
                 st_MM(k + 2)
             if k == -1:
                 nc.tensor.matmul(out=gpn[:], lhsT=nsc_mat[:], rhs=vrow[:, 1, :], start=True, stop=True)
-                nc.tensor.matmul(out=nbp[:], lhsT=nsc_mat[:], rhs=vrow[:, 2, :], start=True, stop=True)
+            if k == NT - 4:
+                cst["nbp"] = psum.tile([P, N], F32, name="nbp", tag="xt", bufs=4)
+                nc.tensor.matmul(out=cst["nbp"][:], lhsT=nsc_mat[:], rhs=vrow[:, 2, :], start=True, stop=True)
             if ok(k + 5):
                 st_T(k + 5)
             if ok(k + 4):
@@ -276,12 +299,11 @@ def tile_modelnew_kernel(tc, x, weight, bias, gamma, beta, scale, out):
             if k + 1 == NB1 - 1:
                 nc.gpsimd.tensor_scalar(out=std[:, 0:NB1], in0=ssq[:, 0:NB1], scalar1=1.0 / N, scalar2=EPS, op0=ALU.mult, op1=ALU.add)
                 nc.gpsimd.tensor_tensor(out=rstd[:, 0:NB1], in0=std[:, 0:NB1], in1=mhalf[:, 0:NB1], op=ALU.pow)
+                nc.gpsimd.tensor_scalar(out=gpn_sb[:], in0=gam_bf[:], scalar1=nscale[:, 0:1], scalar2=0.0, op0=ALU.mult, op1=ALU.add)
+                nc.gpsimd.tensor_scalar(out=nbp_sb[:], in0=bet_bf[:], scalar1=nscale[:, 0:1], scalar2=0.0, op0=ALU.mult, op1=ALU.add)
             if k + 1 == NT - 1:
                 nc.gpsimd.tensor_scalar(out=std[:, NB1:NT], in0=ssq[:, NB1:NT], scalar1=1.0 / N, scalar2=EPS, op0=ALU.mult, op1=ALU.add)
                 nc.gpsimd.tensor_tensor(out=rstd[:, NB1:NT], in0=std[:, NB1:NT], in1=mhalf[:, NB1:NT], op=ALU.pow)
-            if k == 6:
-                nc.gpsimd.tensor_scalar(out=gpn_sb[:], in0=gam_bf[:], scalar1=nscale[:, 0:1], scalar2=0.0, op0=ALU.mult, op1=ALU.add)
-                nc.gpsimd.tensor_scalar(out=nbp_sb[:], in0=bet_bf[:], scalar1=nscale[:, 0:1], scalar2=0.0, op0=ALU.mult, op1=ALU.add)
             if ok(k) and k not in GB:
                 st_B(k)
             if ok(k + 3) and k + 3 >= 1:
@@ -289,17 +311,23 @@ def tile_modelnew_kernel(tc, x, weight, bias, gamma, beta, scale, out):
 
         for i in GB:
             st_BCG(i)
-        for i in range(-1, NT):
-            if ok(i + 1) and i + 1 not in GB:
-                st_C(i + 1)
-            if ok(i):
-                st_D(i)
-                st_E(i)
-            j = i - RL
-            if j >= 1 and j % 2 == 1:
-                st_R(j - 1, 2)
-                st_F(j - 1)
-                st_F(j)
-        for j in range(NT - RL - 1, NT):
-            st_R(j, 1)
-            st_F(j)
+        for q in range(-1, NP):
+            for i in (2 * q + 2, 2 * q + 3):
+                if ok(i) and i not in GB:
+                    st_C(i)
+            if q == NP - 1:
+                for i in (2 * q, 2 * q + 1):
+                    st_D1(i)
+                    st_E(i)
+            elif q >= 0:
+                st_D(q)
+                st_E(2 * q)
+                st_E(2 * q + 1)
+            for r in R_AT.get(q, ()):
+                st_R(2 * r, 2)
+                st_F(2 * r)
+                st_F(2 * r + 1)
+        for r in (NP - 2, NP - 1):
+            st_R(2 * r, 2)
+            st_F(2 * r)
+            st_F(2 * r + 1)

@@ -19,12 +19,15 @@ P = 128
 NT = M // P
 NW = N // P
 G = K // 512
-NB1 = 12
-GB = (13, 14, 15)
-FG = (7, 8, 9, 10, 11)
-FV = (12, 13, 15)
-NP = NT // 2
-R_AT = {2: (0,), 3: (1,), 4: (2, 3), 5: (4,), 6: (5,)}
+TG = ((0, 2, 4, 6), (8, 10, 12, 14))
+TT = TG[0] + TG[1]
+UNITS = ((1, 3), (5, 7), (0, 2), (4, 6), (9, 11), (13, 15), (8, 10), (12, 14))
+ORD = tuple(i for u in UNITS for i in u)
+NB1 = 8
+FG = (1, 3, 5, 7, 0, 2, 4, 6, 9, 11)
+FV = (13, 15, 8, 10, 12, 14)
+YV = ()
+T_AT = {0: 0, 4: 1}
 N_WARM = 4
 N_KEEP = 2
 
@@ -48,19 +51,20 @@ def tile_modelnew_kernel(tc, x, weight, bias, gamma, beta, scale, out):
         ident = const.tile([P, P], F32, name="ident")
         ones = const.tile([P, P], BF16, name="ones")
         vrow = const.tile([P, 3, N], BF16, name="vrow")
+        gbrow = const.tile([P, P], BF16, name="gbrow")
+        sel = const.tile([P, 2 * NW], BF16, name="sel")
+        gbcol = const.tile([P, 2 * NW], F32, name="gbcol")
         srow = const.tile([P, 2], BF16, name="srow")
         nsc_mat = const.tile([P, P], BF16, name="nsc_mat")
         zrow = const.tile([P, N], BF16, name="zrow")
         warm = const.tile([P, 4], F32, name="warm")
         nscale = const.tile([P, 1], F32, name="nscale")
         bias_bc = const.tile([P, N], F32, name="bias_bc")
-        gam_bf = const.tile([P, N], BF16, name="gam_bf")
-        bet_bf = const.tile([P, N], BF16, name="bet_bf")
-        gpn_sb = const.tile([P, N], F32, name="gpn_sb")
-        nbp_sb = const.tile([P, N], F32, name="nbp_sb")
         gpn = pconst.tile([P, N], F32, name="gpn")
+        nbp = pconst.tile([P, N], F32, name="nbp")
         sums = const.tile([P, NT], F32, name="sums")
         negmean = const.tile([P, NT], F32, name="negmean")
+        nmg = const.tile([P, NT], F32, name="nmg")
         ssq = const.tile([P, NT], F32, name="ssq")
         std = const.tile([P, NT], F32, name="std")
         mhalf = const.tile([P, NT], F32, name="mhalf")
@@ -78,6 +82,7 @@ def tile_modelnew_kernel(tc, x, weight, bias, gamma, beta, scale, out):
         nc.vector.memset(warm[:], 0.0)
         nc.vector.memset(mhalf[:], -0.5)
         nc.vector.memset(vrow[:], 0.0)
+        nc.vector.memset(gbrow[:], 0.0)
         make_identity(nc, ident[:])
         nc.scalar.activation(out=warm[:, 1:2], in_=warm[:, 0:1], func=ACT.Exp)
 
@@ -99,10 +104,10 @@ def tile_modelnew_kernel(tc, x, weight, bias, gamma, beta, scale, out):
         nc.sync.dma_start(out=vrow[0:1, 0, :], in_=bias.rearrange("(o n) -> o n", o=1))
         nc.sync.dma_start(out=vrow[0:1, 1, :], in_=gamma.rearrange("(o n) -> o n", o=1))
         nc.sync.dma_start(out=vrow[0:1, 2, :], in_=beta.rearrange("(o n) -> o n", o=1))
+        nc.sync.dma_start(out=gbrow[0:NW, :], in_=gamma.rearrange("(j p) -> j p", p=P))
+        nc.sync.dma_start(out=gbrow[NW:2 * NW, :], in_=beta.rearrange("(j p) -> j p", p=P))
         for i in range(1, NT):
             load_x(i)
-        nc.sync.dma_start(out=gam_bf[:], in_=gamma.partition_broadcast(P))
-        nc.sync.dma_start(out=bet_bf[:], in_=beta.partition_broadcast(P))
 
         xt = {}
         grp = {}
@@ -113,11 +118,16 @@ def tile_modelnew_kernel(tc, x, weight, bias, gamma, beta, scale, out):
         t2 = {}
         sneg = {}
         sp = {}
-        cst = {}
         e = {}
+        zT = {}
+        yT = {}
+        ring = []
+
+        def col(i):
+            return ORD.index(i)
 
         def transposes(src):
-            bank = psum.tile([P, 512], F32, name="xt", tag="xt", bufs=4)
+            bank = psum.tile([P, 512], F32, name="xt", tag="xt")
             words = src[:].bitcast(F32)
             for g in range(G):
                 for u in range(2):
@@ -158,8 +168,8 @@ def tile_modelnew_kernel(tc, x, weight, bias, gamma, beta, scale, out):
                 )
 
         def st_A(i):
-            if i in GB:
-                h[i] = keep.tile([P, N], F32, name="hg", tag="hg", bufs=len(GB))
+            if i in TT:
+                h[i] = keep.tile([P, N], F32, name="hk", tag="hk", bufs=len(TT))
             else:
                 h[i] = work.tile([P, N], F32, name="h", tag="h")
             nc.vector.scalar_tensor_tensor(
@@ -168,71 +178,102 @@ def tile_modelnew_kernel(tc, x, weight, bias, gamma, beta, scale, out):
             )
 
         def st_SQ(i):
-            nc.scalar.mul(out=negmean[:, i:i + 1], in_=sums[:, i:i + 1], mul=-1.0 / N)
+            if i not in TT:
+                nc.scalar.mul(out=negmean[:, i:i + 1], in_=sums[:, i:i + 1], mul=-1.0 / N)
             junk = work.tile([P, N], F32, name="junk", tag="junk", bufs=2)
             nc.scalar.activation(
                 out=junk[:], in_=h[i][:], func=ACT.Square,
-                bias=negmean[:, i:i + 1], scale=1.0, accum_out=ssq[:, i:i + 1],
+                bias=sums[:, i:i + 1], scale=-1.0 * N, accum_out=ssq[:, i:i + 1],
             )
 
+        def st_STD(a, b):
+            nc.gpsimd.tensor_scalar(out=std[:, a:b], in0=ssq[:, a:b], scalar1=1.0 / (N * N * N), scalar2=EPS, op0=ALU.mult, op1=ALU.add)
+            nc.gpsimd.tensor_tensor(out=rstd[:, a:b], in0=std[:, a:b], in1=mhalf[:, a:b], op=ALU.pow)
+            nc.gpsimd.tensor_scalar(out=nmg[:, a:b], in0=sums[:, a:b], scalar1=-1.0 / N, scalar2=0.0, op0=ALU.mult, op1=ALU.add)
+
         def st_B(i):
-            t2[i] = keep.tile([P, N], F32, name="t2", tag="t2")
+            t2[i] = keep.tile([P, N], F32, name="t2", tag="t2", bufs=NT - len(TT))
             nc.vector.scalar_tensor_tensor(
                 out=t2[i][:], in0=h[i][:], scalar=negmean[:, i:i + 1], in1=gpn[:],
                 op0=ALU.add, op1=ALU.mult,
             )
 
-        def new_sneg(i):
-            if i // 2 not in sp:
-                sp[i // 2] = keep.tile([P, 2, N], F32, name="sp", tag="sp", bufs=NP)
-            sneg[i] = sp[i // 2][:, i % 2, :]
-
-        def st_C(i):
-            new_sneg(i)
+        def st_C(u, i):
+            if u not in sp:
+                sp[u] = keep.tile([P, 2, N], F32, name="sp", tag="sp", bufs=4)
+            sneg[i] = sp[u][:, UNITS[u].index(i), :]
             nc.vector.scalar_tensor_tensor(
-                out=sneg[i], in0=t2[i][:], scalar=rstd[:, i:i + 1], in1=cst["nbp"][:],
+                out=sneg[i], in0=t2[i][:], scalar=rstd[:, i:i + 1], in1=nbp[:],
                 op0=ALU.mult, op1=ALU.add,
             )
 
-        def st_BCG(i):
-            new_sneg(i)
-            nc.gpsimd.tensor_scalar(
-                out=sneg[i], in0=h[i][:], scalar1=negmean[:, i:i + 1], scalar2=rstd[:, i:i + 1],
-                op0=ALU.add, op1=ALU.mult,
-            )
-            nc.gpsimd.tensor_tensor(out=sneg[i], in0=sneg[i], in1=gpn_sb[:], op=ALU.mult)
-            nc.gpsimd.tensor_tensor(out=sneg[i], in0=sneg[i], in1=nbp_sb[:], op=ALU.add)
-
-        def st_D(p):
-            nc.vector.tensor_reduce(
-                out=negm[:, 2 * p:2 * p + 2], in_=sp[p][:], axis=mybir.AxisListType.X, op=ALU.min,
-            )
+        def st_D(u):
+            c = 2 * u
+            nc.vector.tensor_reduce(out=negm[:, c:c + 2], in_=sp[u][:], axis=mybir.AxisListType.X, op=ALU.min)
 
         def st_D1(i):
-            nc.vector.tensor_reduce(
-                out=negm[:, i:i + 1], in_=sneg[i], axis=mybir.AxisListType.X, op=ALU.min,
+            c = col(i)
+            nc.vector.tensor_reduce(out=negm[:, c:c + 1], in_=sneg[i], axis=mybir.AxisListType.X, op=ALU.min)
+
+        def bank():
+            tag = ("xt", "acc")[(len(ring) // 3) % 2]
+            ring.append(tag)
+            return psum.tile([P, N], F32, name="bk", tag=tag)
+
+        def st_Z(i):
+            nc.gpsimd.tensor_scalar(
+                out=h[i][:], in0=h[i][:], scalar1=nmg[:, i:i + 1], scalar2=rstd[:, i:i + 1],
+                op0=ALU.add, op1=ALU.mult,
             )
 
-        def st_E(i):
-            e[i] = work.tile([P, N], F32, name="e", tag="e", bufs=12)
-            nc.scalar.activation(
-                out=e[i][:], in_=sneg[i], func=ACT.Exp,
-                bias=negm[:, i:i + 1], scale=-1.0, accum_out=esum[:, i:i + 1],
-            )
+        def st_TZ(g):
+            for j in range(NW):
+                zT[g, j] = bank()
+            for a in range(4):
+                for j in range(NW):
+                    nc.tensor.transpose(zT[g, j][:, a * P:(a + 1) * P], h[TG[g][a]][:, j * P:(j + 1) * P], ident[:])
 
-        def st_R(i, n):
-            nc.vector.reciprocal(out=rsum[:, i:i + n], in_=esum[:, i:i + n])
-
-        def st_F(i):
-            if i in FV:
-                nc.vector.tensor_scalar(out=e[i][:], in0=e[i][:], scalar1=rsum[:, i:i + 1], scalar2=None, op0=ALU.mult)
-            elif i in FG:
-                nc.gpsimd.tensor_scalar(
-                    out=e[i][:], in0=e[i][:], scalar1=rsum[:, i:i + 1], scalar2=0.0,
+        def st_Y(g, j):
+            yT[g, j] = keep.tile([P, N], F32, name="yT", tag="yT", bufs=2 * NW)
+            if (g, j) in YV:
+                nc.vector.tensor_scalar(
+                    out=yT[g, j][:], in0=zT[g, j][:], scalar1=gbcol[:, j:j + 1], scalar2=gbcol[:, NW + j:NW + j + 1],
                     op0=ALU.mult, op1=ALU.add,
                 )
             else:
-                nc.scalar.activation(out=e[i][:], in_=e[i][:], func=ACT.Copy, scale=rsum[:, i:i + 1])
+                nc.scalar.activation(
+                    out=yT[g, j][:], in_=zT[g, j][:], func=ACT.Identity,
+                    scale=gbcol[:, j:j + 1], bias=gbcol[:, NW + j:NW + j + 1],
+                )
+
+        def st_TY(g, a):
+            y = bank()
+            for j in range(NW):
+                nc.tensor.transpose(y[:, j * P:(j + 1) * P], yT[g, j][:, a * P:(a + 1) * P], ident[:])
+            sneg[TG[g][a]] = y[:]
+
+        def st_E(i):
+            c = col(i)
+            e[i] = work.tile([P, N], F32, name="e", tag="e", bufs=12)
+            nc.scalar.activation(
+                out=e[i][:], in_=sneg[i], func=ACT.Exp,
+                bias=negm[:, c:c + 1], scale=-1.0, accum_out=esum[:, c:c + 1],
+            )
+
+        def st_R(u):
+            nc.vector.reciprocal(out=rsum[:, 2 * u:2 * u + 2], in_=esum[:, 2 * u:2 * u + 2])
+
+        def st_F(i):
+            c = col(i)
+            if i in FV:
+                nc.vector.tensor_scalar(out=e[i][:], in0=e[i][:], scalar1=rsum[:, c:c + 1], scalar2=None, op0=ALU.mult)
+            elif i in FG:
+                nc.gpsimd.tensor_scalar(
+                    out=e[i][:], in0=e[i][:], scalar1=rsum[:, c:c + 1], scalar2=0.0,
+                    op0=ALU.mult, op1=ALU.add,
+                )
+            else:
+                nc.scalar.activation(out=e[i][:], in_=e[i][:], func=ACT.Copy, scale=rsum[:, c:c + 1])
             nc.sync.dma_start(out=out_t[i], in_=e[i][:])
 
         def ok(i):
@@ -252,7 +293,7 @@ def tile_modelnew_kernel(tc, x, weight, bias, gamma, beta, scale, out):
             wwords = w_sb[j][:].bitcast(F32)
             wbank = {}
             for g in range(G):
-                wbank[g] = psum.tile([P, 512], F32, name="wt", tag="xt", bufs=4)
+                wbank[g] = psum.tile([P, 512], F32, name="wt", tag="xt")
                 for u in range(2):
                     nc.tensor.transpose(wbank[g][:, u * P:(u + 1) * P], wwords[:, 256 * g + u:256 * (g + 1):2], ident[:])
             nc.scalar.copy(
@@ -275,6 +316,7 @@ def tile_modelnew_kernel(tc, x, weight, bias, gamma, beta, scale, out):
                 nc.tensor.matmul(out=ps_s[:, 0:2], lhsT=ones[:], rhs=srow[:], start=True, stop=True)
                 nc.vector.tensor_scalar(out=nscale[:], in0=ps_s[:, 0:1], scalar1=-1.0, scalar2=None, op0=ALU.mult)
                 nc.vector.tensor_scalar(out=nsc_mat[:], in0=ones[:], scalar1=nscale[:, 0:1], scalar2=None, op0=ALU.mult)
+                nc.vector.tensor_scalar(out=sel[:], in0=ident[:, 0:2 * NW], scalar1=nscale[:, 0:1], scalar2=None, op0=ALU.mult)
                 dummy_mm(N_KEEP)
         ps_b = psum.tile([P, N], F32, name="ps_b", tag="acc")
         nc.tensor.matmul(out=ps_b[:], lhsT=ones[:], rhs=vrow[:, 0, :], start=True, stop=True)
@@ -286,9 +328,11 @@ def tile_modelnew_kernel(tc, x, weight, bias, gamma, beta, scale, out):
                 st_MM(k + 2)
             if k == -1:
                 nc.tensor.matmul(out=gpn[:], lhsT=nsc_mat[:], rhs=vrow[:, 1, :], start=True, stop=True)
-            if k == NT - 4:
-                cst["nbp"] = psum.tile([P, N], F32, name="nbp", tag="xt", bufs=4)
-                nc.tensor.matmul(out=cst["nbp"][:], lhsT=nsc_mat[:], rhs=vrow[:, 2, :], start=True, stop=True)
+                nc.tensor.matmul(out=nbp[:], lhsT=nsc_mat[:], rhs=vrow[:, 2, :], start=True, stop=True)
+            if k == 1:
+                ps_g = psum.tile([P, N], F32, name="ps_g", tag="acc")
+                nc.tensor.matmul(out=ps_g[:, 0:2 * NW], lhsT=gbrow[:], rhs=sel[:], start=True, stop=True)
+                nc.scalar.copy(out=gbcol[:], in_=ps_g[:, 0:2 * NW])
             if ok(k + 5):
                 st_T(k + 5)
             if ok(k + 4):
@@ -297,37 +341,48 @@ def tile_modelnew_kernel(tc, x, weight, bias, gamma, beta, scale, out):
                 st_A(k + 1)
                 st_SQ(k + 1)
             if k + 1 == NB1 - 1:
-                nc.gpsimd.tensor_scalar(out=std[:, 0:NB1], in0=ssq[:, 0:NB1], scalar1=1.0 / N, scalar2=EPS, op0=ALU.mult, op1=ALU.add)
-                nc.gpsimd.tensor_tensor(out=rstd[:, 0:NB1], in0=std[:, 0:NB1], in1=mhalf[:, 0:NB1], op=ALU.pow)
-                nc.gpsimd.tensor_scalar(out=gpn_sb[:], in0=gam_bf[:], scalar1=nscale[:, 0:1], scalar2=0.0, op0=ALU.mult, op1=ALU.add)
-                nc.gpsimd.tensor_scalar(out=nbp_sb[:], in0=bet_bf[:], scalar1=nscale[:, 0:1], scalar2=0.0, op0=ALU.mult, op1=ALU.add)
+                st_STD(0, NB1)
+                for i in TG[0]:
+                    st_Z(i)
             if k + 1 == NT - 1:
-                nc.gpsimd.tensor_scalar(out=std[:, NB1:NT], in0=ssq[:, NB1:NT], scalar1=1.0 / N, scalar2=EPS, op0=ALU.mult, op1=ALU.add)
-                nc.gpsimd.tensor_tensor(out=rstd[:, NB1:NT], in0=std[:, NB1:NT], in1=mhalf[:, NB1:NT], op=ALU.pow)
-            if ok(k) and k not in GB:
+                st_STD(NB1, NT)
+                for i in TG[1]:
+                    st_Z(i)
+            if ok(k) and k not in TT:
                 st_B(k)
             if ok(k + 3) and k + 3 >= 1:
                 st_Q(k + 3)
 
-        for i in GB:
-            st_BCG(i)
-        for q in range(-1, NP):
-            for i in (2 * q + 2, 2 * q + 3):
-                if ok(i) and i not in GB:
-                    st_C(i)
-            if q == NP - 1:
-                for i in (2 * q, 2 * q + 1):
-                    st_D1(i)
+        def t_group(g):
+            st_TZ(g)
+            for j in range(NW):
+                st_Y(g, j)
+            for a in range(4):
+                st_TY(g, a)
+
+        def vmode(u):
+            return u < len(UNITS) and UNITS[u][0] not in TT
+
+        def c_steps(u):
+            for i in UNITS[u]:
+                st_C(u, i)
+
+        c_steps(0)
+        for u in range(len(UNITS) + 2):
+            if u in T_AT:
+                t_group(T_AT[u])
+            if vmode(u + 1):
+                c_steps(u + 1)
+            if u >= 2:
+                st_R(u - 2)
+            if u < len(UNITS):
+                if vmode(u):
+                    st_D(u)
+                else:
+                    for i in UNITS[u]:
+                        st_D1(i)
+                for i in UNITS[u]:
                     st_E(i)
-            elif q >= 0:
-                st_D(q)
-                st_E(2 * q)
-                st_E(2 * q + 1)
-            for r in R_AT.get(q, ()):
-                st_R(2 * r, 2)
-                st_F(2 * r)
-                st_F(2 * r + 1)
-        for r in (NP - 2, NP - 1):
-            st_R(2 * r, 2)
-            st_F(2 * r)
-            st_F(2 * r + 1)
+            if u >= 2:
+                for i in UNITS[u - 2]:
+                    st_F(i)

@@ -23,7 +23,7 @@ TG = ((0, 2, 4, 6), (8, 10, 12, 14))
 TT = TG[0] + TG[1]
 UNITS = ((1, 3), (5, 7), (0, 2), (4, 6), (9, 11), (13, 15), (8, 10), (12, 14))
 ORD = tuple(i for u in UNITS for i in u)
-NB1 = 8
+NB1 = 10
 FG = (1, 3, 5, 7, 0, 2, 4, 6, 9, 11)
 FV = (13, 15, 8, 10, 12, 14)
 YV = ()

@@ -150,8 +150,8 @@ def tile_modelnew_kernel(tc, x, weight, bias, gamma, beta, scale, out):
             )
 
         def st_Q(i):
-            codes[i] = work.tile([P, K // 4], U32, name="codes", tag="codes", align_bytes=64)
-            scl[i] = work.tile([P, K // 4], U8, name="scl", tag="scl", align_bytes=64)
+            codes[i] = work.tile([P, K // 4], U32, name="codes", tag="codes", align_bytes=64, bufs=6)
+            scl[i] = work.tile([P, K // 4], U8, name="scl", tag="scl", align_bytes=64, bufs=6)
             nc.vector.quantize_mx(out=codes[i][:].bitcast(E5X4), scales=scl[i][:], in_=grp[i][:])
 
         def st_MM(i):
@@ -323,20 +323,23 @@ def tile_modelnew_kernel(tc, x, weight, bias, gamma, beta, scale, out):
         nc.vector.tensor_copy(out=bias_bc[:], in_=ps_b[:])
         st_T(1)
 
-        for k in range(-3, NT):
-            if ok(k + 2):
-                st_MM(k + 2)
-            if k == -1:
-                nc.tensor.matmul(out=gpn[:], lhsT=nsc_mat[:], rhs=vrow[:, 1, :], start=True, stop=True)
-                nc.tensor.matmul(out=nbp[:], lhsT=nsc_mat[:], rhs=vrow[:, 2, :], start=True, stop=True)
-            if k == 1:
-                ps_g = psum.tile([P, N], F32, name="ps_g", tag="acc")
+        for k in range(-4, NT):
+            if k % 2 == 0:
+                for i in (k + 2, k + 3):
+                    if ok(i):
+                        st_MM(i)
+                if k == 0:
+                    nc.tensor.matmul(out=gpn[:], lhsT=nsc_mat[:], rhs=vrow[:, 1, :], start=True, stop=True)
+                    nc.tensor.matmul(out=nbp[:], lhsT=nsc_mat[:], rhs=vrow[:, 2, :], start=True, stop=True)
+                for i in (k + 6, k + 7):
+                    if ok(i):
+                        st_T(i)
+            if k == NT - 2:
+                ps_g = psum.tile([P, N], F32, name="ps_g", tag="xt")
                 nc.tensor.matmul(out=ps_g[:, 0:2 * NW], lhsT=gbrow[:], rhs=sel[:], start=True, stop=True)
                 nc.scalar.copy(out=gbcol[:], in_=ps_g[:, 0:2 * NW])
             if ok(k + 5):
-                st_T(k + 5)
-            if ok(k + 4):
-                st_CP(k + 4)
+                st_CP(k + 5)
             if ok(k + 1):
                 st_A(k + 1)
                 st_SQ(k + 1)
@@ -350,8 +353,8 @@ def tile_modelnew_kernel(tc, x, weight, bias, gamma, beta, scale, out):
                     st_Z(i)
             if ok(k) and k not in TT:
                 st_B(k)
-            if ok(k + 3) and k + 3 >= 1:
-                st_Q(k + 3)
+            if ok(k + 4) and k + 4 >= 1:
+                st_Q(k + 4)
 
         def t_group(g):
             st_TZ(g)

@@ -24,8 +24,8 @@ TT = TG[0] + TG[1]
 UNITS = ((1, 3), (5, 7), (0, 2), (4, 6), (9, 11), (13, 15), (8, 10), (12, 14))
 ORD = tuple(i for u in UNITS for i in u)
 NB1 = 10
-FG = (1, 3, 5, 7, 0, 2, 4, 6, 9, 11)
-FV = (13, 15, 8, 10, 12, 14)
+FG = (1, 3, 5, 7, 0, 2, 4, 6, 9, 11, 13, 15)
+FV = (8, 10, 12, 14)
 YV = ()
 T_AT = {0: 0, 4: 1}
 N_WARM = 4

from contextlib import ExitStack

import concourse.mybir as mybir
from concourse.masks import make_identity

M, K, N = 2048, 1024, 512
EPS = 1e-05
FLOPS = 2 * M * K * N

F32 = mybir.dt.float32
BF16 = mybir.dt.bfloat16
U32 = mybir.dt.uint32
U8 = mybir.dt.uint8
E5X4 = mybir.dt.float8_e5m2_x4
ALU = mybir.AluOpType
ACT = mybir.ActivationFunctionType

P = 128
NT = M // P
NW = N // P
G = K // 512
TG = ((0, 2, 4, 6), (8, 10, 12, 14))
TT = TG[0] + TG[1]
UNITS = ((1, 3), (5, 7), (0, 2), (4, 6), (9, 11), (13, 15), (8, 10), (12, 14))
ORD = tuple(i for u in UNITS for i in u)
NB1 = 10
FG = (1, 3, 5, 7, 0, 2, 4, 6, 9, 11, 13, 15)
FV = (8, 10, 12, 14)
YV = ()
T_AT = {0: 0, 4: 1}
N_WARM = 4
N_KEEP = 2


def tile_modelnew_kernel(tc, x, weight, bias, gamma, beta, scale, out):
    nc = tc.nc
    x_t = x.rearrange("(i p) k -> i p k", p=P)
    w_t = weight.rearrange("(j p) k -> j p k", p=P)
    out_t = out.rearrange("(i p) n -> i p n", p=P)

    with ExitStack() as ctx:
        const = ctx.enter_context(tc.tile_pool(name="const", bufs=1))
        xin = ctx.enter_context(tc.tile_pool(name="xin", bufs=NT))
        win = ctx.enter_context(tc.tile_pool(name="win", bufs=NW))
        work = ctx.enter_context(tc.tile_pool(name="work", bufs=4))
        keep = ctx.enter_context(tc.tile_pool(name="keep", bufs=NT))
        psum = ctx.enter_context(tc.psum_pool(name="psum", bufs=3))
        pconst = ctx.enter_context(tc.psum_pool(name="pconst", bufs=1))
        ctx.enter_context(tc.manual_schedule())

        ident = const.tile([P, P], F32, name="ident")
        ones = const.tile([P, P], BF16, name="ones")
        vrow = const.tile([P, 3, N], BF16, name="vrow")
        gbrow = const.tile([P, P], BF16, name="gbrow")
        sel = const.tile([P, 2 * NW], BF16, name="sel")
        gbcol = const.tile([P, 2 * NW], F32, name="gbcol")
        srow = const.tile([P, 2], BF16, name="srow")
        nsc_mat = const.tile([P, P], BF16, name="nsc_mat")
        zrow = const.tile([P, N], BF16, name="zrow")
        warm = const.tile([P, 4], F32, name="warm")
        nscale = const.tile([P, 1], F32, name="nscale")
        bias_bc = const.tile([P, N], F32, name="bias_bc")
        gpn = pconst.tile([P, N], F32, name="gpn")
        nbp = pconst.tile([P, N], F32, name="nbp")
        sums = const.tile([P, NT], F32, name="sums")
        negmean = const.tile([P, NT], F32, name="negmean")
        nmg = const.tile([P, NT], F32, name="nmg")
        ssq = const.tile([P, NT], F32, name="ssq")
        std = const.tile([P, NT], F32, name="std")
        mhalf = const.tile([P, NT], F32, name="mhalf")
        rstd = const.tile([P, NT], F32, name="rstd")
        negm = const.tile([P, NT], F32, name="negm")
        esum = const.tile([P, NT], F32, name="esum")
        rsum = const.tile([P, NT], F32, name="rsum")
        wgrp = const.tile([P, G * N * 4], BF16, name="wgrp", align_bytes=64)
        wcodes = const.tile([P, G * N], U32, name="wcodes", align_bytes=64)
        wscl = const.tile([P, G * N], U8, name="wscl", align_bytes=64)

        nc.vector.memset(ones[:], 1.0)
        nc.vector.memset(zrow[:], 0.0)
        nc.vector.memset(srow[:], 0.0)
        nc.vector.memset(warm[:], 0.0)
        nc.vector.memset(mhalf[:], -0.5)
        nc.vector.memset(vrow[:], 0.0)
        nc.vector.memset(gbrow[:], 0.0)
        make_identity(nc, ident[:])
        nc.scalar.activation(out=warm[:, 1:2], in_=warm[:, 0:1], func=ACT.Exp)

        x_sb = {}
        w_sb = {}

        def load_x(i):
            x_sb[i] = xin.tile([P, K], BF16, name="x_sb", tag="x_sb")
            nc.sync.dma_start(out=x_sb[i][:], in_=x_t[i])

        def load_w(j):
            w_sb[j] = win.tile([P, K], BF16, name="w_sb", tag="w_sb")
            nc.sync.dma_start(out=w_sb[j][:], in_=w_t[j])

        load_x(0)
        nc.sync.dma_start(out=srow[0:1, 0:1], in_=scale.rearrange("(o n) -> o n", o=1))
        for j in range(NW):
            load_w(j)
        nc.sync.dma_start(out=vrow[0:1, 0, :], in_=bias.rearrange("(o n) -> o n", o=1))
        nc.sync.dma_start(out=vrow[0:1, 1, :], in_=gamma.rearrange("(o n) -> o n", o=1))
        nc.sync.dma_start(out=vrow[0:1, 2, :], in_=beta.rearrange("(o n) -> o n", o=1))
        nc.sync.dma_start(out=gbrow[0:NW, :], in_=gamma.rearrange("(j p) -> j p", p=P))
        nc.sync.dma_start(out=gbrow[NW:2 * NW, :], in_=beta.rearrange("(j p) -> j p", p=P))
        for i in range(1, NT):
            load_x(i)

        xt = {}
        grp = {}
        codes = {}
        scl = {}
        acc = {}
        h = {}
        t2 = {}
        sneg = {}
        sp = {}
        e = {}
        zT = {}
        yT = {}
        ring = []

        def col(i):
            return ORD.index(i)

        def transposes(src):
            bank = psum.tile([P, 512], F32, name="xt", tag="xt")
            words = src[:].bitcast(F32)
            for g in range(G):
                for u in range(2):
                    q = 2 * g + u
                    nc.tensor.transpose(
                        bank[:, q * P:(q + 1) * P],
                        words[:, 256 * g + u:256 * (g + 1):2],
                        ident[:],
                    )
            return bank

        def st_T(i):
            xt[i] = transposes(x_sb[i])

        def st_CP(i):
            grp[i] = work.tile([P, K], BF16, name="grp", tag="grp", align_bytes=64)
            nc.scalar.copy(
                out=grp[i][:].bitcast(F32).rearrange("p (g r u) -> p g r u", g=G, u=2),
                in_=xt[i][:].rearrange("p (g u r) -> p g r u", g=G, u=2),
            )

        def st_Q(i):
            codes[i] = work.tile([P, K // 4], U32, name="codes", tag="codes", align_bytes=64, bufs=6)
            scl[i] = work.tile([P, K // 4], U8, name="scl", tag="scl", align_bytes=64, bufs=6)
            nc.vector.quantize_mx(out=codes[i][:].bitcast(E5X4), scales=scl[i][:], in_=grp[i][:])

        def st_MM(i):
            acc[i] = psum.tile([P, N], F32, name="acc", tag="acc")
            for g in range(G):
                nc.tensor.matmul_mx(
                    out=acc[i][:],
                    lhsT=codes[i][:, g * P:(g + 1) * P].bitcast(E5X4),
                    lhsT_scale=scl[i][:, g * P:(g + 1) * P],
                    rhs=wcodes[:, g * N:(g + 1) * N].bitcast(E5X4),
                    rhs_scale=wscl[:, g * N:(g + 1) * N],
                    start=(g == 0),
                    stop=(g == G - 1),
                )

        def st_A(i):
            if i in TT:
                h[i] = keep.tile([P, N], F32, name="hk", tag="hk", bufs=len(TT))
            else:
                h[i] = work.tile([P, N], F32, name="h", tag="h")
            nc.vector.scalar_tensor_tensor(
                out=h[i][:], in0=acc[i][:], scalar=1.0, in1=bias_bc[:],
                op0=ALU.mult, op1=ALU.add, accum_out=sums[:, i:i + 1],
            )

        def st_SQ(i):
            if i not in TT:
                nc.scalar.mul(out=negmean[:, i:i + 1], in_=sums[:, i:i + 1], mul=-1.0 / N)
            junk = work.tile([P, N], F32, name="junk", tag="junk", bufs=2)
            nc.scalar.activation(
                out=junk[:], in_=h[i][:], func=ACT.Square,
                bias=sums[:, i:i + 1], scale=-1.0 * N, accum_out=ssq[:, i:i + 1],
            )

        def st_STD(a, b):
            nc.gpsimd.tensor_scalar(out=std[:, a:b], in0=ssq[:, a:b], scalar1=1.0 / (N * N * N), scalar2=EPS, op0=ALU.mult, op1=ALU.add)
            nc.gpsimd.tensor_tensor(out=rstd[:, a:b], in0=std[:, a:b], in1=mhalf[:, a:b], op=ALU.pow)
            nc.gpsimd.tensor_scalar(out=nmg[:, a:b], in0=sums[:, a:b], scalar1=-1.0 / N, scalar2=0.0, op0=ALU.mult, op1=ALU.add)

        def st_B(i):
            t2[i] = keep.tile([P, N], F32, name="t2", tag="t2", bufs=NT - len(TT))
            nc.vector.scalar_tensor_tensor(
                out=t2[i][:], in0=h[i][:], scalar=negmean[:, i:i + 1], in1=gpn[:],
                op0=ALU.add, op1=ALU.mult,
            )

        def st_C(u, i):
            if u not in sp:
                sp[u] = keep.tile([P, 2, N], F32, name="sp", tag="sp", bufs=4)
            sneg[i] = sp[u][:, UNITS[u].index(i), :]
            nc.vector.scalar_tensor_tensor(
                out=sneg[i], in0=t2[i][:], scalar=rstd[:, i:i + 1], in1=nbp[:],
                op0=ALU.mult, op1=ALU.add,
            )

        def st_D(u):
            c = 2 * u
            nc.vector.tensor_reduce(out=negm[:, c:c + 2], in_=sp[u][:], axis=mybir.AxisListType.X, op=ALU.min)

        def st_D1(i):
            c = col(i)
            nc.vector.tensor_reduce(out=negm[:, c:c + 1], in_=sneg[i], axis=mybir.AxisListType.X, op=ALU.min)

        def bank():
            tag = ("xt", "acc")[(len(ring) // 3) % 2]
            ring.append(tag)
            return psum.tile([P, N], F32, name="bk", tag=tag)

        def st_Z(i):
            nc.gpsimd.tensor_scalar(
                out=h[i][:], in0=h[i][:], scalar1=nmg[:, i:i + 1], scalar2=rstd[:, i:i + 1],
                op0=ALU.add, op1=ALU.mult,
            )

        def st_TZ(g):
            for j in range(NW):
                zT[g, j] = bank()
            for a in range(4):
                for j in range(NW):
                    nc.tensor.transpose(zT[g, j][:, a * P:(a + 1) * P], h[TG[g][a]][:, j * P:(j + 1) * P], ident[:])

        def st_Y(g, j):
            yT[g, j] = keep.tile([P, N], F32, name="yT", tag="yT", bufs=2 * NW)
            if (g, j) in YV:
                nc.vector.tensor_scalar(
                    out=yT[g, j][:], in0=zT[g, j][:], scalar1=gbcol[:, j:j + 1], scalar2=gbcol[:, NW + j:NW + j + 1],
                    op0=ALU.mult, op1=ALU.add,
                )
            else:
                nc.scalar.activation(
                    out=yT[g, j][:], in_=zT[g, j][:], func=ACT.Identity,
                    scale=gbcol[:, j:j + 1], bias=gbcol[:, NW + j:NW + j + 1],
                )

        def st_TY(g, a):
            y = bank()
            for j in range(NW):
                nc.tensor.transpose(y[:, j * P:(j + 1) * P], yT[g, j][:, a * P:(a + 1) * P], ident[:])
            sneg[TG[g][a]] = y[:]

        def st_E(i):
            c = col(i)
            e[i] = work.tile([P, N], F32, name="e", tag="e", bufs=12)
            nc.scalar.activation(
                out=e[i][:], in_=sneg[i], func=ACT.Exp,
                bias=negm[:, c:c + 1], scale=-1.0, accum_out=esum[:, c:c + 1],
            )

        def st_R(u):
            nc.vector.reciprocal(out=rsum[:, 2 * u:2 * u + 2], in_=esum[:, 2 * u:2 * u + 2])

        def st_F(i):
            c = col(i)
            if i in FV:
                nc.vector.tensor_scalar(out=e[i][:], in0=e[i][:], scalar1=rsum[:, c:c + 1], scalar2=None, op0=ALU.mult)
            elif i in FG:
                nc.gpsimd.tensor_scalar(
                    out=e[i][:], in0=e[i][:], scalar1=rsum[:, c:c + 1], scalar2=0.0,
                    op0=ALU.mult, op1=ALU.add,
                )
            else:
                nc.scalar.activation(out=e[i][:], in_=e[i][:], func=ACT.Copy, scale=rsum[:, c:c + 1])
            nc.sync.dma_start(out=out_t[i], in_=e[i][:])

        def ok(i):
            return 0 <= i < NT

        def dummy_mm(n):
            for d in range(n):
                ps_d = psum.tile([P, N], F32, name="ps_d", tag="acc")
                nc.tensor.matmul(out=ps_d[:], lhsT=ones[:], rhs=zrow[:], start=True, stop=True)

        dummy_mm(N_WARM)
        st_T(0)
        st_CP(0)
        st_Q(0)
        wgrp_w = wgrp[:].bitcast(F32).rearrange("p (g c u) -> p g c u", g=G, u=2)
        for j in range(NW):
            wwords = w_sb[j][:].bitcast(F32)
            wbank = {}
            for g in range(G):
                wbank[g] = psum.tile([P, 512], F32, name="wt", tag="xt")
                for u in range(2):
                    nc.tensor.transpose(wbank[g][:, u * P:(u + 1) * P], wwords[:, 256 * g + u:256 * (g + 1):2], ident[:])
            nc.scalar.copy(
                out=wgrp_w[:, 0, j * P:(j + 1) * P, :],
                in_=wbank[0][:, 0:2 * P].rearrange("p (u r) -> p r u", u=2),
            )
            nc.vector.tensor_copy(
                out=wgrp_w[:, 1, j * P:(j + 1) * P, :],
                in_=wbank[1][:, 0:2 * P].rearrange("p (u r) -> p r u", u=2),
            )
            for g in range(G):
                c0 = g * N + j * P
                nc.vector.quantize_mx(
                    out=wcodes[:, c0:c0 + P].bitcast(E5X4),
                    scales=wscl[:, c0:c0 + P],
                    in_=wgrp[:, 4 * c0:4 * (c0 + P)],
                )
            if j == 1:
                ps_s = psum.tile([P, N], F32, name="ps_s", tag="acc")
                nc.tensor.matmul(out=ps_s[:, 0:2], lhsT=ones[:], rhs=srow[:], start=True, stop=True)
                nc.vector.tensor_scalar(out=nscale[:], in0=ps_s[:, 0:1], scalar1=-1.0, scalar2=None, op0=ALU.mult)
                nc.vector.tensor_scalar(out=nsc_mat[:], in0=ones[:], scalar1=nscale[:, 0:1], scalar2=None, op0=ALU.mult)
                nc.vector.tensor_scalar(out=sel[:], in0=ident[:, 0:2 * NW], scalar1=nscale[:, 0:1], scalar2=None, op0=ALU.mult)
                dummy_mm(N_KEEP)
        ps_b = psum.tile([P, N], F32, name="ps_b", tag="acc")
        nc.tensor.matmul(out=ps_b[:], lhsT=ones[:], rhs=vrow[:, 0, :], start=True, stop=True)
        nc.vector.tensor_copy(out=bias_bc[:], in_=ps_b[:])
        st_T(1)

        for k in range(-4, NT):
            if k % 2 == 0:
                for i in (k + 2, k + 3):
                    if ok(i):
                        st_MM(i)
                if k == 0:
                    nc.tensor.matmul(out=gpn[:], lhsT=nsc_mat[:], rhs=vrow[:, 1, :], start=True, stop=True)
                    nc.tensor.matmul(out=nbp[:], lhsT=nsc_mat[:], rhs=vrow[:, 2, :], start=True, stop=True)
                for i in (k + 6, k + 7):
                    if ok(i):
                        st_T(i)
            if k == NT - 2:
                ps_g = psum.tile([P, N], F32, name="ps_g", tag="xt")
                nc.tensor.matmul(out=ps_g[:, 0:2 * NW], lhsT=gbrow[:], rhs=sel[:], start=True, stop=True)
                nc.scalar.copy(out=gbcol[:], in_=ps_g[:, 0:2 * NW])
            if ok(k + 5):
                st_CP(k + 5)
            if ok(k + 1):
                st_A(k + 1)
                st_SQ(k + 1)
            if k + 1 == NB1 - 1:
                st_STD(0, NB1)
                for i in TG[0]:
                    st_Z(i)
            if k + 1 == NT - 1:
                st_STD(NB1, NT)
                for i in TG[1]:
                    st_Z(i)
            if ok(k) and k not in TT:
                st_B(k)
            if ok(k + 4) and k + 4 >= 1:
                st_Q(k + 4)

        def t_group(g):
            st_TZ(g)
            for j in range(NW):
                st_Y(g, j)
            for a in range(4):
                st_TY(g, a)

        def vmode(u):
            return u < len(UNITS) and UNITS[u][0] not in TT

        def c_steps(u):
            for i in UNITS[u]:
                st_C(u, i)

        c_steps(0)
        for u in range(len(UNITS) + 2):
            if u in T_AT:
                t_group(T_AT[u])
            if vmode(u + 1):
                c_steps(u + 1)
            if u >= 2:
                st_R(u - 2)
            if u < len(UNITS):
                if vmode(u):
                    st_D(u)
                else:
                    for i in UNITS[u]:
                        st_D1(i)
                for i in UNITS[u]:
                    st_E(i)
            if u >= 2:
                for i in UNITS[u - 2]:
                    st_F(i)
